import numpy as np
import ml_dtypes

BF16 = ml_dtypes.bfloat16


def bf(x):
    return np.asarray(x, np.float32).astype(BF16)


def f32(x):
    return np.asarray(x, np.float32)


def f64(x):
    return np.asarray(x).astype(np.float64)


def striped(idx):
    return np.tile(idx.reshape(-1, 16).T, (8, 1))


BT, NC, C, S, ND, HALF, K, N = 256, 2, 512, 1024, 4, 512, 8, 4096
H00, H01, H10, H11 = 1.0, 0.25, -0.5, 0.75


def setup_inputs():
    idx = np.concatenate([np.random.permutation(S)[:HALF] for _ in range(K)])
    return {"x": f32(np.random.standard_normal((C, S))), "offs": striped(idx)}


def reference(x, offs):
    idx = offs[:16].T.reshape(-1)
    xv = f64(x)
    x0, x1 = xv[:BT], xv[BT:]
    y = np.concatenate([H00 * x0 + H10 * x1, H01 * x0 + H11 * x1], axis=0)
    prod = xv[:, idx] * np.tile(y, (1, ND))
    return prod[:BT] + prod[BT:]

@@ -1,0 +1,48 @@
+import concourse.mybir as mybir
+
+F32 = mybir.dt.float32
+U16 = mybir.dt.uint16
+MULT = mybir.AluOpType.mult
+ADD = mybir.AluOpType.add
+
+P = 128
+SAMPLES = 256
+NODES = 1024
+DIRECTIONS = 4
+H00, H01, H10, H11 = 1.0, 0.25, -0.5, 0.75
+PIECE_COLUMNS = NODES // 16
+
+
+def tile_gaugenet_kernel(tc, x, offs, out):
+    nc = tc.nc
+    assert H00 == 1.0
+    with (
+        tc.tile_pool(name="held", bufs=1) as held,
+        tc.tile_pool(name="work", bufs=2) as work,
+    ):
+        offsets = held.tile([P, DIRECTIONS * PIECE_COLUMNS], U16, name="offsets")
+        nc.sync.dma_start(offsets[:], offs)
+
+        for block in range(SAMPLES // P):
+            rows = slice(block * P, (block + 1) * P)
+            x0 = held.tile([P, NODES], F32, name=f"x0_{block}")
+            x1 = held.tile([P, NODES], F32, name=f"x1_{block}")
+            nc.sync.dma_start(x0[:], x[block * P : (block + 1) * P, :])
+            nc.scalar.dma_start(x1[:], x[SAMPLES + block * P : SAMPLES + (block + 1) * P, :])
+
+            y0 = held.tile([P, NODES], F32, name=f"y0_{block}")
+            y1 = held.tile([P, NODES], F32, name=f"y1_{block}")
+            scaled = work.tile([P, NODES], F32, name="scaled")
+            nc.vector.scalar_tensor_tensor(y0[:], x1[:], H10, x0[:], MULT, ADD)
+            nc.scalar.mul(scaled[:], x0[:], H01)
+            nc.vector.scalar_tensor_tensor(y1[:], x1[:], H11, scaled[:], MULT, ADD)
+
+            for direction in range(DIRECTIONS):
+                piece = offsets[:, direction * PIECE_COLUMNS : (direction + 1) * PIECE_COLUMNS]
+                product0 = work.tile([P, NODES], F32, name="product0")
+                product1 = work.tile([P, NODES], F32, name="product1")
+                links = work.tile([P, NODES], F32, name="links")
+                nc.vector.tensor_tensor(product0[:], x0[:].indirect(piece), y0[:], MULT)
+                nc.vector.tensor_tensor(product1[:], x1[:].indirect(piece), y1[:], MULT)
+                nc.vector.tensor_tensor(links[:], product0[:], product1[:], ADD)
+                nc.sync.dma_start(out[rows, direction * NODES : (direction + 1) * NODES], links[:])

@@ -1,4 +1,5 @@
 import concourse.mybir as mybir
+from concourse.masks import make_identity
 
 F32 = mybir.dt.float32
 U16 = mybir.dt.uint16
@@ -11,6 +12,7 @@ NODES = 1024
 DIRECTIONS = 4
 H00, H01, H10, H11 = 1.0, 0.25, -0.5, 0.75
 PIECE_COLUMNS = NODES // 16
+BANK = 512
 
 
 def tile_gaugenet_kernel(tc, x, offs, out):
@@ -18,13 +20,15 @@ def tile_gaugenet_kernel(tc, x, offs, out):
     assert H00 == 1.0
     with (
         tc.tile_pool(name="held", bufs=1) as held,
-        tc.tile_pool(name="work", bufs=2) as work,
+        tc.tile_pool(name="work", bufs=3) as work,
+        tc.psum_pool(name="psum", bufs=2) as psum,
     ):
         offsets = held.tile([P, DIRECTIONS * PIECE_COLUMNS], U16, name="offsets")
         nc.sync.dma_start(offsets[:], offs)
+        identity = held.tile([P, P], F32, name="identity")
+        make_identity(nc, identity[:])
 
         for block in range(SAMPLES // P):
-            rows = slice(block * P, (block + 1) * P)
             x0 = held.tile([P, NODES], F32, name=f"x0_{block}")
             x1 = held.tile([P, NODES], F32, name=f"x1_{block}")
             nc.sync.dma_start(x0[:], x[block * P : (block + 1) * P, :])
@@ -41,8 +45,17 @@ def tile_gaugenet_kernel(tc, x, offs, out):
                 piece = offsets[:, direction * PIECE_COLUMNS : (direction + 1) * PIECE_COLUMNS]
                 product0 = work.tile([P, NODES], F32, name="product0")
                 product1 = work.tile([P, NODES], F32, name="product1")
-                links = work.tile([P, NODES], F32, name="links")
                 nc.vector.tensor_tensor(product0[:], x0[:].indirect(piece), y0[:], MULT)
                 nc.vector.tensor_tensor(product1[:], x1[:].indirect(piece), y1[:], MULT)
-                nc.vector.tensor_tensor(links[:], product0[:], product1[:], ADD)
-                nc.sync.dma_start(out[rows, direction * NODES : (direction + 1) * NODES], links[:])
+
+                halves = [slice(h * BANK, (h + 1) * BANK) for h in range(NODES // BANK)]
+                banks = [psum.tile([P, BANK], F32, name=f"bank{h}") for h in range(NODES // BANK)]
+                links = work.tile([P, NODES], F32, name="links")
+                for bank, half in zip(banks, halves):
+                    nc.tensor.matmul(bank[:], identity[:], product0[:, half], start=True, stop=False)
+                for bank, half in zip(banks, halves):
+                    nc.tensor.matmul(bank[:], identity[:], product1[:, half], start=False, stop=True)
+                    nc.scalar.copy(links[:, half], bank[:])
+                nc.sync.dma_start(
+                    out[block * P : (block + 1) * P, direction * NODES : (direction + 1) * NODES], links[:]
+                )

@@ -8,11 +8,14 @@ ADD = mybir.AluOpType.add
 
 P = 128
 SAMPLES = 256
+BLOCKS = SAMPLES // P
 NODES = 1024
 DIRECTIONS = 4
 H00, H01, H10, H11 = 1.0, 0.25, -0.5, 0.75
-PIECE_COLUMNS = NODES // 16
 BANK = 512
+HALVES = [slice(h * BANK, (h + 1) * BANK) for h in range(NODES // BANK)]
+DIRECTION_RUNS = [(direction * NODES, NODES) for direction in range(DIRECTIONS)]
+LAST_BLOCK_RUNS = DIRECTION_RUNS[:-1] + [((DIRECTIONS - 1) * NODES + h * BANK, BANK) for h in range(NODES // BANK)]
 
 
 def tile_gaugenet_kernel(tc, x, offs, out):
@@ -23,39 +26,46 @@ def tile_gaugenet_kernel(tc, x, offs, out):
         tc.tile_pool(name="work", bufs=3) as work,
         tc.psum_pool(name="psum", bufs=2) as psum,
     ):
-        offsets = held.tile([P, DIRECTIONS * PIECE_COLUMNS], U16, name="offsets")
+        offsets = held.tile([P, DIRECTIONS * NODES // 16], U16, name="offsets")
         nc.sync.dma_start(offsets[:], offs)
         identity = held.tile([P, P], F32, name="identity")
         make_identity(nc, identity[:])
 
-        for block in range(SAMPLES // P):
-            x0 = held.tile([P, NODES], F32, name=f"x0_{block}")
-            x1 = held.tile([P, NODES], F32, name=f"x1_{block}")
-            nc.sync.dma_start(x0[:], x[block * P : (block + 1) * P, :])
-            nc.scalar.dma_start(x1[:], x[SAMPLES + block * P : SAMPLES + (block + 1) * P, :])
+        x0 = [held.tile([P, NODES], F32, name=f"x0_{block}") for block in range(BLOCKS)]
+        x1 = [held.tile([P, NODES], F32, name=f"x1_{block}") for block in range(BLOCKS)]
+        for block in range(BLOCKS):
+            for half in HALVES:
+                nc.sync.dma_start(x0[block][:, half], x[block * P : (block + 1) * P, half])
+                nc.scalar.dma_start(x1[block][:, half], x[SAMPLES + block * P : SAMPLES + (block + 1) * P, half])
 
+        identity_h01 = held.tile([P, P], F32, name="identity_h01")
+        nc.scalar.mul(identity_h01[:], identity[:], H01)
+
+        for block in range(BLOCKS):
             y0 = held.tile([P, NODES], F32, name=f"y0_{block}")
             y1 = held.tile([P, NODES], F32, name=f"y1_{block}")
-            scaled = work.tile([P, NODES], F32, name="scaled")
-            nc.vector.scalar_tensor_tensor(y0[:], x1[:], H10, x0[:], MULT, ADD)
-            nc.scalar.mul(scaled[:], x0[:], H01)
-            nc.vector.scalar_tensor_tensor(y1[:], x1[:], H11, scaled[:], MULT, ADD)
+            for half in HALVES:
+                nc.vector.scalar_tensor_tensor(y0[:, half], x1[block][:, half], H10, x0[block][:, half], MULT, ADD)
+                nc.vector.scalar_tensor_tensor(y1[:, half], x1[block][:, half], H11 / H01, x0[block][:, half], MULT, ADD)
 
-            for direction in range(DIRECTIONS):
-                piece = offsets[:, direction * PIECE_COLUMNS : (direction + 1) * PIECE_COLUMNS]
-                product0 = work.tile([P, NODES], F32, name="product0")
-                product1 = work.tile([P, NODES], F32, name="product1")
-                nc.vector.tensor_tensor(product0[:], x0[:].indirect(piece), y0[:], MULT)
-                nc.vector.tensor_tensor(product1[:], x1[:].indirect(piece), y1[:], MULT)
+            last_block = block == BLOCKS - 1
+            for first, length in LAST_BLOCK_RUNS if last_block else DIRECTION_RUNS:
+                piece = offsets[:, first // 16 : (first + length) // 16]
+                nodes = slice(first % NODES, first % NODES + length)
+                product0 = work.tile([P, length], F32, name="product0")
+                product1 = work.tile([P, length], F32, name="product1")
+                links = work.tile([P, length], F32, name="links")
+                nc.vector.tensor_tensor(product0[:], x0[block][:].indirect(piece), y0[:, nodes], MULT)
+                nc.vector.tensor_tensor(product1[:], x1[block][:].indirect(piece), y1[:, nodes], MULT)
 
-                halves = [slice(h * BANK, (h + 1) * BANK) for h in range(NODES // BANK)]
-                banks = [psum.tile([P, BANK], F32, name=f"bank{h}") for h in range(NODES // BANK)]
-                links = work.tile([P, NODES], F32, name="links")
-                for bank, half in zip(banks, halves):
-                    nc.tensor.matmul(bank[:], identity[:], product0[:, half], start=True, stop=False)
-                for bank, half in zip(banks, halves):
-                    nc.tensor.matmul(bank[:], identity[:], product1[:, half], start=False, stop=True)
-                    nc.scalar.copy(links[:, half], bank[:])
-                nc.sync.dma_start(
-                    out[block * P : (block + 1) * P, direction * NODES : (direction + 1) * NODES], links[:]
-                )
+                if last_block and first + length == DIRECTIONS * NODES:
+                    nc.vector.scalar_tensor_tensor(links[:], product1[:], H01, product0[:], MULT, ADD)
+                else:
+                    columns = [slice(c, c + BANK) for c in range(0, length, BANK)]
+                    banks = [psum.tile([P, BANK], F32, name=f"bank{i}") for i in range(len(columns))]
+                    for bank, part in zip(banks, columns):
+                        nc.tensor.matmul(bank[:], identity[:], product0[:, part], start=True, stop=False)
+                    for bank, part in zip(banks, columns):
+                        nc.tensor.matmul(bank[:], identity_h01[:], product1[:, part], start=False, stop=True)
+                        nc.scalar.copy(links[:, part], bank[:])
+                nc.sync.dma_start(out[block * P : (block + 1) * P, first : first + length], links[:])

@@ -13,7 +13,8 @@ NODES = 1024
 DIRECTIONS = 4
 H00, H01, H10, H11 = 1.0, 0.25, -0.5, 0.75
 BANK = 512
-HALVES = [slice(h * BANK, (h + 1) * BANK) for h in range(NODES // BANK)]
+PART = 256
+FIRST_BLOCK_PARTS = [slice(c, c + PART) for c in range(0, NODES, PART)]
 DIRECTION_RUNS = [(direction * NODES, NODES) for direction in range(DIRECTIONS)]
 LAST_BLOCK_RUNS = DIRECTION_RUNS[:-1] + [((DIRECTIONS - 1) * NODES + h * BANK, BANK) for h in range(NODES // BANK)]
 
@@ -26,17 +27,19 @@ def tile_gaugenet_kernel(tc, x, offs, out):
         tc.tile_pool(name="work", bufs=3) as work,
         tc.psum_pool(name="psum", bufs=2) as psum,
     ):
-        offsets = held.tile([P, DIRECTIONS * NODES // 16], U16, name="offsets")
-        nc.sync.dma_start(offsets[:], offs)
         identity = held.tile([P, P], F32, name="identity")
         make_identity(nc, identity[:])
 
         x0 = [held.tile([P, NODES], F32, name=f"x0_{block}") for block in range(BLOCKS)]
         x1 = [held.tile([P, NODES], F32, name=f"x1_{block}") for block in range(BLOCKS)]
-        for block in range(BLOCKS):
-            for half in HALVES:
-                nc.sync.dma_start(x0[block][:, half], x[block * P : (block + 1) * P, half])
-                nc.scalar.dma_start(x1[block][:, half], x[SAMPLES + block * P : SAMPLES + (block + 1) * P, half])
+        offsets = held.tile([P, DIRECTIONS * NODES // 16], U16, name="offsets")
+        for part in FIRST_BLOCK_PARTS:
+            nc.sync.dma_start(x0[0][:, part], x[0:P, part])
+            nc.sync.dma_start(x1[0][:, part], x[SAMPLES : SAMPLES + P, part])
+        nc.sync.dma_start(offsets[:], offs)
+        for block in range(1, BLOCKS):
+            nc.sync.dma_start(x0[block][:], x[block * P : (block + 1) * P, :])
+            nc.sync.dma_start(x1[block][:], x[SAMPLES + block * P : SAMPLES + (block + 1) * P, :])
 
         identity_h01 = held.tile([P, P], F32, name="identity_h01")
         nc.scalar.mul(identity_h01[:], identity[:], H01)
@@ -44,9 +47,9 @@ def tile_gaugenet_kernel(tc, x, offs, out):
         for block in range(BLOCKS):
             y0 = held.tile([P, NODES], F32, name=f"y0_{block}")
             y1 = held.tile([P, NODES], F32, name=f"y1_{block}")
-            for half in HALVES:
-                nc.vector.scalar_tensor_tensor(y0[:, half], x1[block][:, half], H10, x0[block][:, half], MULT, ADD)
-                nc.vector.scalar_tensor_tensor(y1[:, half], x1[block][:, half], H11 / H01, x0[block][:, half], MULT, ADD)
+            for part in FIRST_BLOCK_PARTS if block == 0 else [slice(0, NODES)]:
+                nc.vector.scalar_tensor_tensor(y0[:, part], x1[block][:, part], H10, x0[block][:, part], MULT, ADD)
+                nc.vector.scalar_tensor_tensor(y1[:, part], x1[block][:, part], H11 / H01, x0[block][:, part], MULT, ADD)
 
             last_block = block == BLOCKS - 1
             for first, length in LAST_BLOCK_RUNS if last_block else DIRECTION_RUNS:

@@ -7,16 +7,19 @@ MULT = mybir.AluOpType.mult
 ADD = mybir.AluOpType.add
 
 P = 128
+HALF_P = P // 2
 SAMPLES = 256
-BLOCKS = SAMPLES // P
 NODES = 1024
 DIRECTIONS = 4
 H00, H01, H10, H11 = 1.0, 0.25, -0.5, 0.75
 BANK = 512
 PART = 256
-FIRST_BLOCK_PARTS = [slice(c, c + PART) for c in range(0, NODES, PART)]
-DIRECTION_RUNS = [(direction * NODES, NODES) for direction in range(DIRECTIONS)]
-LAST_BLOCK_RUNS = DIRECTION_RUNS[:-1] + [((DIRECTIONS - 1) * NODES + h * BANK, BANK) for h in range(NODES // BANK)]
+LAST = (DIRECTIONS - 1) * NODES
+STEPS = (
+    [(0, direction * NODES, NODES) for direction in range(DIRECTIONS - 1)]
+    + [(1, direction * NODES, NODES) for direction in range(DIRECTIONS)]
+    + [(0, LAST, BANK), (0, LAST + BANK, BANK)]
+)
 
 
 def tile_gaugenet_kernel(tc, x, offs, out):
@@ -24,51 +27,69 @@ def tile_gaugenet_kernel(tc, x, offs, out):
     assert H00 == 1.0
     with (
         tc.tile_pool(name="held", bufs=1) as held,
+        tc.tile_pool(name="products", bufs=2) as product_pool,
         tc.tile_pool(name="work", bufs=3) as work,
-        tc.psum_pool(name="psum", bufs=2) as psum,
+        tc.psum_pool(name="psum", bufs=4) as psum,
     ):
+        windows = [[held.tile([P, NODES], F32, name=f"x_{block}_{t}") for t in range(2)] for block in range(2)]
+        ys = [[held.tile([P, NODES], F32, name=f"y_{block}_{t}") for t in range(2)] for block in range(2)]
+        offsets = held.tile([P, DIRECTIONS * NODES // 16], U16, name="offsets")
+
+        parts = [slice(c, c + PART) for c in range(0, NODES, PART)]
+        for part in parts:
+            nc.sync.dma_start(windows[0][0][:, part], x[0:P, part])
+            nc.sync.dma_start(windows[0][1][:, part], x[SAMPLES : SAMPLES + P, part])
+        nc.sync.dma_start(offsets[:], offs)
+        for t in range(2):
+            first_sample = P + t * HALF_P
+            nc.sync.dma_start(windows[1][t][:HALF_P, :], x[first_sample : first_sample + HALF_P, :])
+            nc.sync.dma_start(windows[1][t][HALF_P:, :], x[SAMPLES + first_sample : SAMPLES + first_sample + HALF_P, :])
+
         identity = held.tile([P, P], F32, name="identity")
         make_identity(nc, identity[:])
-
-        x0 = [held.tile([P, NODES], F32, name=f"x0_{block}") for block in range(BLOCKS)]
-        x1 = [held.tile([P, NODES], F32, name=f"x1_{block}") for block in range(BLOCKS)]
-        offsets = held.tile([P, DIRECTIONS * NODES // 16], U16, name="offsets")
-        for part in FIRST_BLOCK_PARTS:
-            nc.sync.dma_start(x0[0][:, part], x[0:P, part])
-            nc.sync.dma_start(x1[0][:, part], x[SAMPLES : SAMPLES + P, part])
-        nc.sync.dma_start(offsets[:], offs)
-        for block in range(1, BLOCKS):
-            nc.sync.dma_start(x0[block][:], x[block * P : (block + 1) * P, :])
-            nc.sync.dma_start(x1[block][:], x[SAMPLES + block * P : SAMPLES + (block + 1) * P, :])
-
+        left, right = identity[:, :HALF_P], identity[:, HALF_P:]
         identity_h01 = held.tile([P, P], F32, name="identity_h01")
         nc.scalar.mul(identity_h01[:], identity[:], H01)
+        scaled_right = held.tile([P, P], F32, name="scaled_right")
+        nc.scalar.mul(scaled_right[:, :HALF_P], right, H10)
+        nc.scalar.mul(scaled_right[:, HALF_P:], right, H11)
+        mix = held.tile([P, P], F32, name="mix")
+        nc.gpsimd.tensor_tensor(mix[:, :HALF_P], left, scaled_right[:, :HALF_P], ADD)
+        nc.gpsimd.tensor_tensor(mix[:, HALF_P:], identity_h01[:, :HALF_P], scaled_right[:, HALF_P:], ADD)
+        folds = held.tile([P, 3 * HALF_P], F32, name="folds")
+        nc.gpsimd.memset(folds[:, HALF_P : 2 * HALF_P], 0.0)
+        nc.gpsimd.tensor_tensor(folds[:, :HALF_P], left, right, ADD)
+        nc.gpsimd.tensor_tensor(folds[:, 2 * HALF_P :], left, right, ADD)
+        adders = [[identity[:], identity_h01[:]], [folds[:, :P], folds[:, HALF_P:]]]
 
-        for block in range(BLOCKS):
-            y0 = held.tile([P, NODES], F32, name=f"y0_{block}")
-            y1 = held.tile([P, NODES], F32, name=f"y1_{block}")
-            for part in FIRST_BLOCK_PARTS if block == 0 else [slice(0, NODES)]:
-                nc.vector.scalar_tensor_tensor(y0[:, part], x1[block][:, part], H10, x0[block][:, part], MULT, ADD)
-                nc.vector.scalar_tensor_tensor(y1[:, part], x1[block][:, part], H11 / H01, x0[block][:, part], MULT, ADD)
+        for part in parts:
+            x0_part, x1_part = windows[0][0][:, part], windows[0][1][:, part]
+            nc.vector.scalar_tensor_tensor(ys[0][0][:, part], x1_part, H10, x0_part, MULT, ADD)
+            nc.vector.scalar_tensor_tensor(ys[0][1][:, part], x1_part, H11 / H01, x0_part, MULT, ADD)
+        for t in range(2):
+            for c in range(0, NODES, BANK):
+                y_bank = psum.tile([P, BANK], F32, name="bank")
+                nc.tensor.matmul(y_bank[:], mix[:], windows[1][t][:, c : c + BANK], start=True, stop=True)
+                nc.scalar.copy(ys[1][t][:, c : c + BANK], y_bank[:])
 
-            last_block = block == BLOCKS - 1
-            for first, length in LAST_BLOCK_RUNS if last_block else DIRECTION_RUNS:
-                piece = offsets[:, first // 16 : (first + length) // 16]
-                nodes = slice(first % NODES, first % NODES + length)
-                product0 = work.tile([P, length], F32, name="product0")
-                product1 = work.tile([P, length], F32, name="product1")
-                links = work.tile([P, length], F32, name="links")
-                nc.vector.tensor_tensor(product0[:], x0[block][:].indirect(piece), y0[:, nodes], MULT)
-                nc.vector.tensor_tensor(product1[:], x1[block][:].indirect(piece), y1[:, nodes], MULT)
-
-                if last_block and first + length == DIRECTIONS * NODES:
-                    nc.vector.scalar_tensor_tensor(links[:], product1[:], H01, product0[:], MULT, ADD)
-                else:
-                    columns = [slice(c, c + BANK) for c in range(0, length, BANK)]
-                    banks = [psum.tile([P, BANK], F32, name=f"bank{i}") for i in range(len(columns))]
-                    for bank, part in zip(banks, columns):
-                        nc.tensor.matmul(bank[:], identity[:], product0[:, part], start=True, stop=False)
-                    for bank, part in zip(banks, columns):
-                        nc.tensor.matmul(bank[:], identity_h01[:], product1[:, part], start=False, stop=True)
-                        nc.scalar.copy(links[:, part], bank[:])
-                nc.sync.dma_start(out[block * P : (block + 1) * P, first : first + length], links[:])
+        for step, (block, first, length) in enumerate(STEPS):
+            piece = offsets[:, first // 16 : (first + length) // 16]
+            nodes = slice(first % NODES, first % NODES + length)
+            rows = out[block * P : (block + 1) * P, first : first + length]
+            in_psum = BANK if step == 0 else 0 if first >= LAST and block == 0 else length
+            products = [product_pool.tile([P, length], F32, name=f"product{t}") for t in range(2)]
+            links = work.tile([P, length], F32, name="links")
+            banks = [psum.tile([P, BANK], F32, name="bank") for c in range(0, in_psum, BANK)]
+            for t in range(2):
+                nc.vector.tensor_tensor(products[t][:], windows[block][t][:].indirect(piece), ys[block][t][:, nodes], MULT)
+                for i, bank in enumerate(banks):
+                    columns = slice(i * BANK, (i + 1) * BANK)
+                    nc.tensor.matmul(bank[:], adders[block][t], products[t][:, columns], start=(t == 0), stop=(t == 1))
+            for i, bank in enumerate(banks):
+                nc.scalar.copy(links[:, i * BANK : (i + 1) * BANK], bank[:])
+            if in_psum > 0:
+                nc.sync.dma_start(rows[:, :in_psum], links[:, :in_psum])
+            for c in range(in_psum, length, PART):
+                part = slice(c, c + PART)
+                nc.vector.scalar_tensor_tensor(links[:, part], products[1][:, part], H01, products[0][:, part], MULT, ADD)
+                nc.sync.dma_start(rows[:, part], links[:, part])

@@ -47,19 +47,19 @@ def tile_gaugenet_kernel(tc, x, offs, out):
 
         identity = held.tile([P, P], F32, name="identity")
         make_identity(nc, identity[:])
-        left, right = identity[:, :HALF_P], identity[:, HALF_P:]
+        upper, lower = identity[:HALF_P, :HALF_P], identity[HALF_P:, HALF_P:]
+        mix = held.tile([P, P], F32, name="mix")
+        nc.scalar.mul(mix[:HALF_P, :HALF_P], upper, H00)
+        nc.scalar.mul(mix[HALF_P:, :HALF_P], lower, H10)
+        nc.scalar.mul(mix[:HALF_P, HALF_P:], upper, H01)
+        nc.scalar.mul(mix[HALF_P:, HALF_P:], lower, H11)
         identity_h01 = held.tile([P, P], F32, name="identity_h01")
         nc.scalar.mul(identity_h01[:], identity[:], H01)
-        scaled_right = held.tile([P, P], F32, name="scaled_right")
-        nc.scalar.mul(scaled_right[:, :HALF_P], right, H10)
-        nc.scalar.mul(scaled_right[:, HALF_P:], right, H11)
-        mix = held.tile([P, P], F32, name="mix")
-        nc.gpsimd.tensor_tensor(mix[:, :HALF_P], left, scaled_right[:, :HALF_P], ADD)
-        nc.gpsimd.tensor_tensor(mix[:, HALF_P:], identity_h01[:, :HALF_P], scaled_right[:, HALF_P:], ADD)
         folds = held.tile([P, 3 * HALF_P], F32, name="folds")
         nc.gpsimd.memset(folds[:, HALF_P : 2 * HALF_P], 0.0)
-        nc.gpsimd.tensor_tensor(folds[:, :HALF_P], left, right, ADD)
-        nc.gpsimd.tensor_tensor(folds[:, 2 * HALF_P :], left, right, ADD)
+        for c in (0, 2 * HALF_P):
+            nc.scalar.copy(folds[:HALF_P, c : c + HALF_P], upper)
+            nc.scalar.copy(folds[HALF_P:, c : c + HALF_P], lower)
         adders = [[identity[:], identity_h01[:]], [folds[:, :P], folds[:, HALF_P:]]]
 
         for part in parts:
@@ -76,7 +76,7 @@ def tile_gaugenet_kernel(tc, x, offs, out):
             piece = offsets[:, first // 16 : (first + length) // 16]
             nodes = slice(first % NODES, first % NODES + length)
             rows = out[block * P : (block + 1) * P, first : first + length]
-            in_psum = BANK if step == 0 else 0 if first >= LAST and block == 0 else length
+            in_psum = BANK if step == 0 else 0 if step == len(STEPS) - 1 else length
             products = [product_pool.tile([P, length], F32, name=f"product{t}") for t in range(2)]
             links = work.tile([P, length], F32, name="links")
             banks = [psum.tile([P, BANK], F32, name="bank") for c in range(0, in_psum, BANK)]

@@ -36,14 +36,15 @@ def tile_gaugenet_kernel(tc, x, offs, out):
         offsets = held.tile([P, DIRECTIONS * NODES // 16], U16, name="offsets")
 
         parts = [slice(c, c + PART) for c in range(0, NODES, PART)]
+        split_rows = x.rearrange("(c p two) n -> two c p n", c=2, two=2)[1]
+        stacked_rows = x.rearrange("(p four) n -> four p n", four=4)
         for part in parts:
-            nc.sync.dma_start(windows[0][0][:, part], x[0:P, part])
-            nc.sync.dma_start(windows[0][1][:, part], x[SAMPLES : SAMPLES + P, part])
+            for component in range(2):
+                nc.sync.dma_start(windows[0][component][:, part], split_rows[component][:, part])
         nc.sync.dma_start(offsets[:], offs)
         for t in range(2):
-            first_sample = P + t * HALF_P
-            nc.sync.dma_start(windows[1][t][:HALF_P, :], x[first_sample : first_sample + HALF_P, :])
-            nc.sync.dma_start(windows[1][t][HALF_P:, :], x[SAMPLES + first_sample : SAMPLES + first_sample + HALF_P, :])
+            nc.sync.dma_start(windows[1][t][:], stacked_rows[2 * t])
+        out_rows = out.rearrange("(p two) j -> two p j", two=2)
 
         identity = held.tile([P, P], F32, name="identity")
         make_identity(nc, identity[:])
@@ -55,12 +56,12 @@ def tile_gaugenet_kernel(tc, x, offs, out):
         nc.scalar.mul(mix[HALF_P:, HALF_P:], lower, H11)
         identity_h01 = held.tile([P, P], F32, name="identity_h01")
         nc.scalar.mul(identity_h01[:], identity[:], H01)
-        folds = held.tile([P, 3 * HALF_P], F32, name="folds")
-        nc.gpsimd.memset(folds[:, HALF_P : 2 * HALF_P], 0.0)
-        for c in (0, 2 * HALF_P):
-            nc.scalar.copy(folds[:HALF_P, c : c + HALF_P], upper)
-            nc.scalar.copy(folds[HALF_P:, c : c + HALF_P], lower)
-        adders = [[identity[:], identity_h01[:]], [folds[:, :P], folds[:, HALF_P:]]]
+        folds = [held.tile([P, P], F32, name=f"fold_{t}") for t in range(2)]
+        for t in range(2):
+            nc.gpsimd.memset(folds[t][:], 0.0)
+            nc.scalar.copy(folds[t][:HALF_P, t::2], upper)
+            nc.scalar.copy(folds[t][HALF_P:, t::2], lower)
+        adders = [[identity[:], identity_h01[:]], [folds[0][:], folds[1][:]]]
 
         for part in parts:
             x0_part, x1_part = windows[0][0][:, part], windows[0][1][:, part]
@@ -75,7 +76,7 @@ def tile_gaugenet_kernel(tc, x, offs, out):
         for step, (block, first, length) in enumerate(STEPS):
             piece = offsets[:, first // 16 : (first + length) // 16]
             nodes = slice(first % NODES, first % NODES + length)
-            rows = out[block * P : (block + 1) * P, first : first + length]
+            rows = out_rows[1 - block][:, first : first + length]
             in_psum = BANK if step == 0 else 0 if step == len(STEPS) - 1 else length
             products = [product_pool.tile([P, length], F32, name=f"product{t}") for t in range(2)]
             links = work.tile([P, length], F32, name="links")

@@ -8,6 +8,7 @@ ADD = mybir.AluOpType.add
 
 P = 128
 HALF_P = P // 2
+STRIP = 32
 SAMPLES = 256
 NODES = 1024
 DIRECTIONS = 4
@@ -44,7 +45,8 @@ def tile_gaugenet_kernel(tc, x, offs, out):
         nc.sync.dma_start(offsets[:], offs)
         for t in range(2):
             nc.sync.dma_start(windows[1][t][:], stacked_rows[2 * t])
-        out_rows = out.rearrange("(p two) j -> two p j", two=2)
+        split_out = out.rearrange("(p two) j -> two p j", two=2)[1]
+        stacked_out = out.rearrange("(m four) j -> four m j", four=4)
 
         identity = held.tile([P, P], F32, name="identity")
         make_identity(nc, identity[:])
@@ -56,12 +58,10 @@ def tile_gaugenet_kernel(tc, x, offs, out):
         nc.scalar.mul(mix[HALF_P:, HALF_P:], lower, H11)
         identity_h01 = held.tile([P, P], F32, name="identity_h01")
         nc.scalar.mul(identity_h01[:], identity[:], H01)
-        folds = [held.tile([P, P], F32, name=f"fold_{t}") for t in range(2)]
-        for t in range(2):
-            nc.gpsimd.memset(folds[t][:], 0.0)
-            nc.scalar.copy(folds[t][:HALF_P, t::2], upper)
-            nc.scalar.copy(folds[t][HALF_P:, t::2], lower)
-        adders = [[identity[:], identity_h01[:]], [folds[0][:], folds[1][:]]]
+        fold = held.tile([P, HALF_P], F32, name="fold")
+        nc.scalar.copy(fold[:HALF_P, :], upper)
+        nc.scalar.copy(fold[HALF_P:, :], lower)
+        adders = [identity[:], identity_h01[:]]
 
         for part in parts:
             x0_part, x1_part = windows[0][0][:, part], windows[0][1][:, part]
@@ -76,21 +76,38 @@ def tile_gaugenet_kernel(tc, x, offs, out):
         for step, (block, first, length) in enumerate(STEPS):
             piece = offsets[:, first // 16 : (first + length) // 16]
             nodes = slice(first % NODES, first % NODES + length)
-            rows = out_rows[1 - block][:, first : first + length]
-            in_psum = BANK if step == 0 else 0 if step == len(STEPS) - 1 else length
             products = [product_pool.tile([P, length], F32, name=f"product{t}") for t in range(2)]
             links = work.tile([P, length], F32, name="links")
-            banks = [psum.tile([P, BANK], F32, name="bank") for c in range(0, in_psum, BANK)]
             for t in range(2):
                 nc.vector.tensor_tensor(products[t][:], windows[block][t][:].indirect(piece), ys[block][t][:, nodes], MULT)
+            if block == 1:
+                for t in range(2):
+                    bank = psum.tile([P, BANK], F32, name="bank")
+                    for column in range(0, P, STRIP):
+                        half, sample = divmod(column, HALF_P)
+                        nc.tensor.matmul(
+                            bank[column : column + STRIP, :],
+                            fold[:, sample : sample + STRIP],
+                            products[t][:, half * BANK : (half + 1) * BANK],
+                            start=True,
+                            stop=True,
+                        )
+                    sums = links[:, t * BANK : (t + 1) * BANK]
+                    nc.scalar.copy(sums, bank[:])
+                    for half in range(2):
+                        columns = slice(first + half * BANK, first + (half + 1) * BANK)
+                        nc.sync.dma_start(stacked_out[2 * t][:, columns], sums[half * HALF_P : (half + 1) * HALF_P, :])
+            elif step < len(STEPS) - 1:
+                banks = [psum.tile([P, BANK], F32, name="bank") for c in range(0, length, BANK)]
+                for t in range(2):
+                    for i, bank in enumerate(banks):
+                        columns = slice(i * BANK, (i + 1) * BANK)
+                        nc.tensor.matmul(bank[:], adders[t], products[t][:, columns], start=(t == 0), stop=(t == 1))
                 for i, bank in enumerate(banks):
-                    columns = slice(i * BANK, (i + 1) * BANK)
-                    nc.tensor.matmul(bank[:], adders[block][t], products[t][:, columns], start=(t == 0), stop=(t == 1))
-            for i, bank in enumerate(banks):
-                nc.scalar.copy(links[:, i * BANK : (i + 1) * BANK], bank[:])
-            if in_psum > 0:
-                nc.sync.dma_start(rows[:, :in_psum], links[:, :in_psum])
-            for c in range(in_psum, length, PART):
-                part = slice(c, c + PART)
-                nc.vector.scalar_tensor_tensor(links[:, part], products[1][:, part], H01, products[0][:, part], MULT, ADD)
-                nc.sync.dma_start(rows[:, part], links[:, part])
+                    nc.scalar.copy(links[:, i * BANK : (i + 1) * BANK], bank[:])
+                nc.sync.dma_start(split_out[:, first : first + length], links[:])
+            else:
+                for c in range(0, length, PART):
+                    part = slice(c, c + PART)
+                    nc.vector.scalar_tensor_tensor(links[:, part], products[1][:, part], H01, products[0][:, part], MULT, ADD)
+                    nc.sync.dma_start(split_out[:, first + c : first + c + PART], links[:, part])

@@ -45,7 +45,7 @@ def tile_gaugenet_kernel(tc, x, offs, out):
         nc.sync.dma_start(offsets[:], offs)
         for t in range(2):
             nc.sync.dma_start(windows[1][t][:], stacked_rows[2 * t])
-        split_out = out.rearrange("(p two) j -> two p j", two=2)[1]
+        out_rows = out.rearrange("(p two) j -> two p j", two=2)
         stacked_out = out.rearrange("(m four) j -> four m j", four=4)
 
         identity = held.tile([P, P], F32, name="identity")
@@ -58,10 +58,15 @@ def tile_gaugenet_kernel(tc, x, offs, out):
         nc.scalar.mul(mix[HALF_P:, HALF_P:], lower, H11)
         identity_h01 = held.tile([P, P], F32, name="identity_h01")
         nc.scalar.mul(identity_h01[:], identity[:], H01)
+        folds = [held.tile([P, P], F32, name=f"fold_{t}") for t in range(2)]
+        for t in range(2):
+            nc.gpsimd.memset(folds[t][:], 0.0)
+            nc.scalar.copy(folds[t][:HALF_P, t::2], upper)
+            nc.scalar.copy(folds[t][HALF_P:, t::2], lower)
         fold = held.tile([P, HALF_P], F32, name="fold")
         nc.scalar.copy(fold[:HALF_P, :], upper)
         nc.scalar.copy(fold[HALF_P:, :], lower)
-        adders = [identity[:], identity_h01[:]]
+        adders = [[identity[:], identity_h01[:]], [folds[0][:], folds[1][:]]]
 
         for part in parts:
             x0_part, x1_part = windows[0][0][:, part], windows[0][1][:, part]
@@ -76,11 +81,12 @@ def tile_gaugenet_kernel(tc, x, offs, out):
         for step, (block, first, length) in enumerate(STEPS):
             piece = offsets[:, first // 16 : (first + length) // 16]
             nodes = slice(first % NODES, first % NODES + length)
+            rows = out_rows[1 - block][:, first : first + length]
             products = [product_pool.tile([P, length], F32, name=f"product{t}") for t in range(2)]
             links = work.tile([P, length], F32, name="links")
             for t in range(2):
                 nc.vector.tensor_tensor(products[t][:], windows[block][t][:].indirect(piece), ys[block][t][:, nodes], MULT)
-            if block == 1:
+            if (block, first) == (1, 0):
                 for t in range(2):
                     bank = psum.tile([P, BANK], F32, name="bank")
                     for column in range(0, P, STRIP):
@@ -102,12 +108,12 @@ def tile_gaugenet_kernel(tc, x, offs, out):
                 for t in range(2):
                     for i, bank in enumerate(banks):
                         columns = slice(i * BANK, (i + 1) * BANK)
-                        nc.tensor.matmul(bank[:], adders[t], products[t][:, columns], start=(t == 0), stop=(t == 1))
+                        nc.tensor.matmul(bank[:], adders[block][t], products[t][:, columns], start=(t == 0), stop=(t == 1))
                 for i, bank in enumerate(banks):
                     nc.scalar.copy(links[:, i * BANK : (i + 1) * BANK], bank[:])
-                nc.sync.dma_start(split_out[:, first : first + length], links[:])
+                nc.sync.dma_start(rows, links[:])
             else:
                 for c in range(0, length, PART):
                     part = slice(c, c + PART)
                     nc.vector.scalar_tensor_tensor(links[:, part], products[1][:, part], H01, products[0][:, part], MULT, ADD)
-                    nc.sync.dma_start(split_out[:, first + c : first + c + PART], links[:, part])
+                    nc.sync.dma_start(rows[:, part], links[:, part])

@@ -79,14 +79,21 @@ def tile_gaugenet_kernel(tc, x, offs, out):
                 nc.scalar.copy(ys[1][t][:, c : c + BANK], y_bank[:])
 
         for step, (block, first, length) in enumerate(STEPS):
-            piece = offsets[:, first // 16 : (first + length) // 16]
-            nodes = slice(first % NODES, first % NODES + length)
             rows = out_rows[1 - block][:, first : first + length]
             products = [product_pool.tile([P, length], F32, name=f"product{t}") for t in range(2)]
             links = work.tile([P, length], F32, name="links")
-            for t in range(2):
-                nc.vector.tensor_tensor(products[t][:], windows[block][t][:].indirect(piece), ys[block][t][:, nodes], MULT)
-            if (block, first) == (1, 0):
+            halves = 2 if step == len(STEPS) - 1 else 1
+            for t, runs in enumerate((1, halves)):
+                run = length // runs
+                for c in range(0, length, run):
+                    start = first + c
+                    nc.vector.tensor_tensor(
+                        products[t][:, c : c + run],
+                        windows[block][t][:].indirect(offsets[:, start // 16 : (start + run) // 16]),
+                        ys[block][t][:, start % NODES : start % NODES + run],
+                        MULT,
+                    )
+            if block == 1 and first in (0, LAST):
                 for t in range(2):
                     bank = psum.tile([P, BANK], F32, name="bank")
                     for column in range(0, P, STRIP):
@@ -111,7 +118,8 @@ def tile_gaugenet_kernel(tc, x, offs, out):
                         nc.tensor.matmul(bank[:], adders[block][t], products[t][:, columns], start=(t == 0), stop=(t == 1))
                 for i, bank in enumerate(banks):
                     nc.scalar.copy(links[:, i * BANK : (i + 1) * BANK], bank[:])
-                nc.sync.dma_start(rows, links[:])
+                queue = nc.scalar if step == len(STEPS) - 2 else nc.sync
+                queue.dma_start(rows, links[:])
             else:
                 for c in range(0, length, PART):
                     part = slice(c, c + PART)

@@ -51,6 +51,8 @@ def tile_gaugenet_kernel(tc, x, offs, out):
         identity = held.tile([P, P], F32, name="identity")
         make_identity(nc, identity[:])
         upper, lower = identity[:HALF_P, :HALF_P], identity[HALF_P:, HALF_P:]
+        identity_ratio = held.tile([P, P], F32, name="identity_ratio")
+        nc.scalar.mul(identity_ratio[:], identity[:], H11 / H01)
         mix = held.tile([P, P], F32, name="mix")
         nc.scalar.mul(mix[:HALF_P, :HALF_P], upper, H00)
         nc.scalar.mul(mix[HALF_P:, :HALF_P], lower, H10)
@@ -68,10 +70,16 @@ def tile_gaugenet_kernel(tc, x, offs, out):
         nc.scalar.copy(fold[HALF_P:, :], lower)
         adders = [[identity[:], identity_h01[:]], [folds[0][:], folds[1][:]]]
 
-        for part in parts:
+        for i, part in enumerate(parts):
             x0_part, x1_part = windows[0][0][:, part], windows[0][1][:, part]
             nc.vector.scalar_tensor_tensor(ys[0][0][:, part], x1_part, H10, x0_part, MULT, ADD)
-            nc.vector.scalar_tensor_tensor(ys[0][1][:, part], x1_part, H11 / H01, x0_part, MULT, ADD)
+            if i == 0:
+                y_bank = psum.tile([P, BANK], F32, name="bank")
+                nc.tensor.matmul(y_bank[:, :PART], identity[:], x0_part, start=True, stop=False)
+                nc.tensor.matmul(y_bank[:, :PART], identity_ratio[:], x1_part, start=False, stop=True)
+                nc.scalar.copy(ys[0][1][:, part], y_bank[:, :PART])
+            else:
+                nc.vector.scalar_tensor_tensor(ys[0][1][:, part], x1_part, H11 / H01, x0_part, MULT, ADD)
         for t in range(2):
             for c in range(0, NODES, BANK):
                 y_bank = psum.tile([P, BANK], F32, name="bank")
@@ -93,7 +101,7 @@ def tile_gaugenet_kernel(tc, x, offs, out):
                         ys[block][t][:, start % NODES : start % NODES + run],
                         MULT,
                     )
-            if block == 1 and first in (0, LAST):
+            if block == 1 and first == LAST:
                 for t in range(2):
                     bank = psum.tile([P, BANK], F32, name="bank")
                     for column in range(0, P, STRIP):

@@ -39,9 +39,11 @@ def tile_gaugenet_kernel(tc, x, offs, out):
         parts = [slice(c, c + PART) for c in range(0, NODES, PART)]
         split_rows = x.rearrange("(c p two) n -> two c p n", c=2, two=2)[1]
         stacked_rows = x.rearrange("(p four) n -> four p n", four=4)
-        for part in parts:
-            for component in range(2):
-                nc.sync.dma_start(windows[0][component][:, part], split_rows[component][:, part])
+        early, late = parts[: len(parts) // 2], parts[len(parts) // 2 :]
+        block_0_loads = [(0, slice(0, NODES // 2))] + [(1, part) for part in early]
+        block_0_loads += [(component, part) for part in late for component in range(2)]
+        for component, columns in block_0_loads:
+            nc.sync.dma_start(windows[0][component][:, columns], split_rows[component][:, columns])
         nc.sync.dma_start(offsets[:], offs)
         for t in range(2):
             nc.sync.dma_start(windows[1][t][:], stacked_rows[2 * t])

import concourse.mybir as mybir
from concourse.masks import make_identity

F32 = mybir.dt.float32
U16 = mybir.dt.uint16
MULT = mybir.AluOpType.mult
ADD = mybir.AluOpType.add

P = 128
HALF_P = P // 2
STRIP = 32
SAMPLES = 256
NODES = 1024
DIRECTIONS = 4
H00, H01, H10, H11 = 1.0, 0.25, -0.5, 0.75
BANK = 512
PART = 256
LAST = (DIRECTIONS - 1) * NODES
STEPS = (
    [(0, direction * NODES, NODES) for direction in range(DIRECTIONS - 1)]
    + [(1, direction * NODES, NODES) for direction in range(DIRECTIONS)]
    + [(0, LAST, BANK), (0, LAST + BANK, BANK)]
)


def tile_gaugenet_kernel(tc, x, offs, out):
    nc = tc.nc
    assert H00 == 1.0
    with (
        tc.tile_pool(name="held", bufs=1) as held,
        tc.tile_pool(name="products", bufs=2) as product_pool,
        tc.tile_pool(name="work", bufs=3) as work,
        tc.psum_pool(name="psum", bufs=4) as psum,
    ):
        windows = [[held.tile([P, NODES], F32, name=f"x_{block}_{t}") for t in range(2)] for block in range(2)]
        ys = [[held.tile([P, NODES], F32, name=f"y_{block}_{t}") for t in range(2)] for block in range(2)]
        offsets = held.tile([P, DIRECTIONS * NODES // 16], U16, name="offsets")

        parts = [slice(c, c + PART) for c in range(0, NODES, PART)]
        split_rows = x.rearrange("(c p two) n -> two c p n", c=2, two=2)[1]
        stacked_rows = x.rearrange("(p four) n -> four p n", four=4)
        early, late = parts[: len(parts) // 2], parts[len(parts) // 2 :]
        block_0_loads = [(0, slice(0, NODES // 2))] + [(1, part) for part in early]
        block_0_loads += [(component, part) for part in late for component in range(2)]
        for component, columns in block_0_loads:
            nc.sync.dma_start(windows[0][component][:, columns], split_rows[component][:, columns])
        nc.sync.dma_start(offsets[:], offs)
        for t in range(2):
            nc.sync.dma_start(windows[1][t][:], stacked_rows[2 * t])
        out_rows = out.rearrange("(p two) j -> two p j", two=2)
        stacked_out = out.rearrange("(m four) j -> four m j", four=4)

        identity = held.tile([P, P], F32, name="identity")
        make_identity(nc, identity[:])
        upper, lower = identity[:HALF_P, :HALF_P], identity[HALF_P:, HALF_P:]
        identity_ratio = held.tile([P, P], F32, name="identity_ratio")
        nc.scalar.mul(identity_ratio[:], identity[:], H11 / H01)
        mix = held.tile([P, P], F32, name="mix")
        nc.scalar.mul(mix[:HALF_P, :HALF_P], upper, H00)
        nc.scalar.mul(mix[HALF_P:, :HALF_P], lower, H10)
        nc.scalar.mul(mix[:HALF_P, HALF_P:], upper, H01)
        nc.scalar.mul(mix[HALF_P:, HALF_P:], lower, H11)
        identity_h01 = held.tile([P, P], F32, name="identity_h01")
        nc.scalar.mul(identity_h01[:], identity[:], H01)
        folds = [held.tile([P, P], F32, name=f"fold_{t}") for t in range(2)]
        for t in range(2):
            nc.gpsimd.memset(folds[t][:], 0.0)
            nc.scalar.copy(folds[t][:HALF_P, t::2], upper)
            nc.scalar.copy(folds[t][HALF_P:, t::2], lower)
        fold = held.tile([P, HALF_P], F32, name="fold")
        nc.scalar.copy(fold[:HALF_P, :], upper)
        nc.scalar.copy(fold[HALF_P:, :], lower)
        adders = [[identity[:], identity_h01[:]], [folds[0][:], folds[1][:]]]

        for i, part in enumerate(parts):
            x0_part, x1_part = windows[0][0][:, part], windows[0][1][:, part]
            nc.vector.scalar_tensor_tensor(ys[0][0][:, part], x1_part, H10, x0_part, MULT, ADD)
            if i == 0:
                y_bank = psum.tile([P, BANK], F32, name="bank")
                nc.tensor.matmul(y_bank[:, :PART], identity[:], x0_part, start=True, stop=False)
                nc.tensor.matmul(y_bank[:, :PART], identity_ratio[:], x1_part, start=False, stop=True)
                nc.scalar.copy(ys[0][1][:, part], y_bank[:, :PART])
            else:
                nc.vector.scalar_tensor_tensor(ys[0][1][:, part], x1_part, H11 / H01, x0_part, MULT, ADD)
        for t in range(2):
            for c in range(0, NODES, BANK):
                y_bank = psum.tile([P, BANK], F32, name="bank")
                nc.tensor.matmul(y_bank[:], mix[:], windows[1][t][:, c : c + BANK], start=True, stop=True)
                nc.scalar.copy(ys[1][t][:, c : c + BANK], y_bank[:])

        for step, (block, first, length) in enumerate(STEPS):
            rows = out_rows[1 - block][:, first : first + length]
            products = [product_pool.tile([P, length], F32, name=f"product{t}") for t in range(2)]
            links = work.tile([P, length], F32, name="links")
            halves = 2 if step == len(STEPS) - 1 else 1
            for t, runs in enumerate((1, halves)):
                run = length // runs
                for c in range(0, length, run):
                    start = first + c
                    nc.vector.tensor_tensor(
                        products[t][:, c : c + run],
                        windows[block][t][:].indirect(offsets[:, start // 16 : (start + run) // 16]),
                        ys[block][t][:, start % NODES : start % NODES + run],
                        MULT,
                    )
            if block == 1 and first == LAST:
                for t in range(2):
                    bank = psum.tile([P, BANK], F32, name="bank")
                    for column in range(0, P, STRIP):
                        half, sample = divmod(column, HALF_P)
                        nc.tensor.matmul(
                            bank[column : column + STRIP, :],
                            fold[:, sample : sample + STRIP],
                            products[t][:, half * BANK : (half + 1) * BANK],
                            start=True,
                            stop=True,
                        )
                    sums = links[:, t * BANK : (t + 1) * BANK]
                    nc.scalar.copy(sums, bank[:])
                    for half in range(2):
                        columns = slice(first + half * BANK, first + (half + 1) * BANK)
                        nc.sync.dma_start(stacked_out[2 * t][:, columns], sums[half * HALF_P : (half + 1) * HALF_P, :])
            elif step < len(STEPS) - 1:
                banks = [psum.tile([P, BANK], F32, name="bank") for c in range(0, length, BANK)]
                for t in range(2):
                    for i, bank in enumerate(banks):
                        columns = slice(i * BANK, (i + 1) * BANK)
                        nc.tensor.matmul(bank[:], adders[block][t], products[t][:, columns], start=(t == 0), stop=(t == 1))
                for i, bank in enumerate(banks):
                    nc.scalar.copy(links[:, i * BANK : (i + 1) * BANK], bank[:])
                queue = nc.scalar if step == len(STEPS) - 2 else nc.sync
                queue.dma_start(rows, links[:])
            else:
                for c in range(0, length, PART):
                    part = slice(c, c + PART)
                    nc.vector.scalar_tensor_tensor(links[:, part], products[1][:, part], H01, products[0][:, part], MULT, ADD)
                    nc.sync.dma_start(rows[:, part], links[:, part])
